import numpy as np
import ml_dtypes


def mxq(x, axis, fmt="e4m3"):
    dtype, down = {"e4m3": (ml_dtypes.float8_e4m3fn, 7), "e5m2": (ml_dtypes.float8_e5m2, 14)}[fmt]
    v = np.moveaxis(np.asarray(x, np.float32).astype(ml_dtypes.bfloat16).astype(np.float64), axis, -1)
    blocks = v.reshape(v.shape[:-1] + (-1, 32))
    amax = np.abs(blocks).max(-1, keepdims=True)
    byte = np.maximum(np.where(amax > 0, np.frexp(amax)[1] - 1 + 127, 0) - down, 1)
    scale = np.exp2(byte - 127.0)
    codes = (blocks / scale).astype(np.float32).astype(dtype).astype(np.float64)
    return np.moveaxis((codes * scale).reshape(v.shape), -1, axis)


WIDE = False


def mx_kscale(k):
    if not WIDE:
        return np.ones(k)
    levels = np.array([10, -10, 5, -5, 0])
    a = np.random.permutation(np.resize(levels, k // 512 * 4)).reshape(k // 512, 4)
    idx = np.arange(k)
    return np.exp2(a[idx // 512, idx % 128 // 32])


BF16 = ml_dtypes.bfloat16


def bf(x):
    return np.asarray(x, np.float32).astype(BF16)


def f64(x):
    return np.asarray(x).astype(np.float64)


E2M1 = np.array([0.0, 0.5, 1.0, 1.5, 2.0, 3.0, 4.0, 6.0, -0.0, -0.5, -1.0, -1.5, -2.0, -3.0, -4.0, -6.0])


def pack_weight(w, fmt):
    k, n = w.shape
    w = f64(bf(w)).reshape(k // 32, 32, n)
    amax = np.abs(w).max(1)
    if fmt == "e4m3":
        byte = np.frexp(amax)[1] - 1 + 127 - 7
    else:
        mant, ex = np.frexp(amax / 6.0)
        byte = np.where(mant > 0.5, ex, ex - 1) + 127
    byte = np.clip(np.where(amax > 0, byte, 1), 1, 254)
    scaled = (w * np.exp2(127.0 - byte)[:, None, :]).reshape(k, n).astype(np.float32)
    by_word = np.ascontiguousarray(scaled.reshape(k // 512, 128, 4, n).transpose(0, 1, 3, 2))
    if fmt == "e4m3":
        words = by_word.astype(ml_dtypes.float8_e4m3fn).view(np.uint8)
    else:
        c = by_word.astype(ml_dtypes.float4_e2m1fn).view(np.uint8) & 0xF
        words = c[..., 0::2] | (c[..., 1::2] << 4)
    return np.ascontiguousarray(words), np.ascontiguousarray(byte.astype(np.uint8).reshape(k // 512, 16, n))


def unpack_weight(words, scales, fmt):
    g, p, n, _ = words.shape
    if fmt == "e4m3":
        vals = np.ascontiguousarray(words).view(ml_dtypes.float8_e4m3fn).astype(np.float64)
    else:
        nib = np.empty((g, p, n, 4), np.uint8)
        nib[..., 0::2] = words & 0xF
        nib[..., 1::2] = words >> 4
        vals = E2M1[nib]
    vals = vals * np.repeat(np.exp2(scales.astype(np.float64) - 127.0), 8, axis=1)[..., None]
    return vals.transpose(0, 1, 3, 2).reshape(g * 512, n)

def pack4(w):
    words, scales = pack_weight(w, "e2m1")
    return words.reshape(words.shape[0], 128, -1), scales


def unpack4(words, scales):
    return unpack_weight(words.reshape(words.shape[0], 128, -1, 2), scales, "e2m1")


B, STACK, TUBE, CH, IMG, PATCH, EMBED = 4, 16, 2, 1, 96, 16, 1024
GH = IMG // PATCH
GW = IMG // PATCH
GD = STACK // TUBE
K = TUBE * CH * PATCH * PATCH


def _sincos_1d(dim, pos):
    omega = 1.0 / (10000.0 ** (np.arange(dim // 2, dtype=np.float64) / (dim / 2.0)))
    out = pos[:, None].astype(np.float64) * omega[None, :]
    return np.concatenate([np.sin(out), np.cos(out)], axis=1)


def get_3d_sincos_pos_embed(grid_h, grid_w, grid_depth, embed_dim):
    dim_t = embed_dim // 4
    dim_s = embed_dim - dim_t
    emb_t = _sincos_1d(dim_t, np.arange(grid_depth))
    emb_h = _sincos_1d(dim_s // 2, np.arange(grid_h))
    emb_w = _sincos_1d(dim_s - dim_s // 2, np.arange(grid_w))
    emb_hw = np.concatenate([np.repeat(emb_h, grid_w, axis=0), np.tile(emb_w, (grid_h, 1))], axis=1)
    ns = grid_h * grid_w
    return np.concatenate([np.repeat(emb_t, ns, axis=0), np.tile(emb_hw, (grid_depth, 1))], axis=1)


def setup_inputs():
    s = mx_kscale(K)
    sv = s.reshape(TUBE, CH, PATCH, PATCH)[:, :, None, :, None, :]
    video = np.random.standard_normal((B, GD, TUBE, CH, GH, PATCH, GW, PATCH)) * sv
    w_nk = np.random.standard_normal((EMBED, K)) / np.sqrt(K) / s[None, :]
    words, scales = pack4(np.ascontiguousarray(w_nk.T))
    return {"video": bf(video.reshape(B, STACK, CH, IMG, IMG)),
            "W_words": words,
            "W_scales": scales,
            "b": bf(np.random.standard_normal(EMBED) * 0.3),
            "pos_embed": bf(get_3d_sincos_pos_embed(GH, GW, GD, EMBED)[None])}


def reference(video, W_words, W_scales, b, pos_embed):
    video = f64(video)
    B_, T, C, H, W_ = video.shape
    p = PATCH
    gh, gw = H // p, W_ // p
    ns = gh * gw
    x = video.reshape(B_ * T, C, gh, p, gw, p)
    x = x.transpose(0, 2, 4, 1, 3, 5)
    x = x.reshape(B_, T, ns, C * p * p)
    x = x.reshape(B_, GD, TUBE, ns, C * p * p)
    x = x.transpose(0, 1, 3, 2, 4)
    tubelets = x.reshape(B_, GD * ns, TUBE * C * p * p)
    tokens = (mxq(tubelets, 2, "e4m3") @ unpack4(W_words, W_scales)) + f64(b) + f64(pos_embed)
    return tokens

@@ -1,0 +1,181 @@
+from contextlib import ExitStack
+
+import concourse.mybir as mybir
+from concourse.masks import make_identity
+
+FLOPS = 2 * 1152 * 512 * 1024
+
+BF16 = mybir.dt.bfloat16
+F32 = mybir.dt.float32
+I32 = mybir.dt.int32
+U32 = mybir.dt.uint32
+U8 = mybir.dt.uint8
+FP8X4 = mybir.dt.float8_e4m3fn_x4
+FP4X4 = mybir.dt.float4_e2m1fn_x4
+ADD = mybir.AluOpType.add
+
+P = 128
+PACK = 4
+BATCH = 4
+TUBES = 8
+CLIPS = BATCH * TUBES
+FRAMES = 2
+GRID = 6
+PATCH = 16
+BAND = PATCH * GRID * PATCH
+CELLS = GRID * GRID
+PATCH_ROWS = FRAMES * PATCH
+EMBED = 1024
+N_TILE = 512
+WIDE_CELLS = 16
+TAIL_CELLS = CELLS - 2 * WIDE_CELLS
+ROWS_A = 4
+
+
+def tile_tubeletembedding_kernel(tc, video, W_words, W_scales, b, pos_embed, out):
+    nc = tc.nc
+    with ExitStack() as ctx:
+        keep = ctx.enter_context(tc.tile_pool(name="keep", bufs=1))
+        sort_pool = ctx.enter_context(tc.tile_pool(name="sort", bufs=4))
+        result_pool = ctx.enter_context(tc.tile_pool(name="result", bufs=6))
+        flip_pool = ctx.enter_context(tc.psum_pool(name="flip", bufs=4))
+        acc_pool = ctx.enter_context(tc.psum_pool(name="acc", bufs=4))
+
+        bands = video.rearrange("b f c h w -> (b f c h w)").rearrange(
+            "(x t i r) -> t x i r", x=CLIPS, t=FRAMES, i=GRID, r=BAND
+        )
+        pos_by_cell = pos_embed[0].rearrange("(d c) e -> c d e", c=CELLS)
+        pos_by_tube = pos_embed[0].rearrange("(d c) e -> d c e", c=CELLS)
+        out_by_cell = out.rearrange("b (d c) e -> b c d e", c=CELLS)
+        out_by_clip = out.rearrange("b (d c) e -> (b d) c e", c=CELLS)
+
+        ident = keep.tile([P, P], F32)
+        make_identity(nc, ident[:])
+        ones = keep.tile([P, P], BF16)
+        nc.vector.memset(ones[:], 1.0)
+        bias_rows = keep.tile([P, EMBED], BF16)
+        nc.vector.memset(bias_rows[:], 0.0)
+        w_scales = keep.tile([P, EMBED], U8, align_bytes=64)
+        nc.vector.memset(w_scales[:].bitcast(I32), 0)
+
+        rows_a = keep.tile([P, FRAMES, BAND], BF16)
+        for t in range(FRAMES):
+            nc.sync.dma_start(out=rows_a[:, t, :], in_=bands[t, :, 0:ROWS_A, :])
+        nc.sync.dma_start(out=bias_rows[0:1, :], in_=b.rearrange("(o e) -> o e", o=1))
+        for quadrant in range(4):
+            nc.sync.dma_start(
+                out=w_scales[32 * quadrant : 32 * quadrant + 4, :].bitcast(I32),
+                in_=W_scales[0, 4 * quadrant : 4 * quadrant + 4, :].bitcast(I32),
+            )
+        w_words = keep.tile([P, 2 * EMBED], U8, align_bytes=64)
+        nc.sync.dma_start(out=w_words[:].bitcast(I32), in_=W_words[0].bitcast(I32))
+        pos_wide = []
+        pos_wide.append(keep.tile([P, EMBED], BF16, name="pos_wide0"))
+        nc.sync.dma_start(out=pos_wide[0][:], in_=pos_by_cell[0:WIDE_CELLS])
+        rows_b = keep.tile([P, FRAMES, BAND], BF16)
+        for t in range(FRAMES):
+            for shift in range(2):
+                nc.sync.dma_start(
+                    out=rows_b[shift:P:2, t, 0 : BAND - PATCH * shift],
+                    in_=bands[t, :, ROWS_A:GRID, PATCH * shift : BAND],
+                )
+        pos_wide.append(keep.tile([P, EMBED], BF16, name="pos_wide1"))
+        nc.sync.dma_start(out=pos_wide[1][:], in_=pos_by_cell[WIDE_CELLS : 2 * WIDE_CELLS])
+        pos_tail = keep.tile([P, EMBED], BF16)
+        for batch in range(BATCH):
+            nc.sync.dma_start(
+                out=pos_tail[TUBES * TAIL_CELLS * batch : TUBES * TAIL_CELLS * (batch + 1), :],
+                in_=pos_by_tube[:, 2 * WIDE_CELLS : CELLS, :],
+            )
+
+        bias_all = keep.tile([P, EMBED], F32)
+        for n in range(EMBED // N_TILE):
+            cols = slice(N_TILE * n, N_TILE * (n + 1))
+            spread = acc_pool.tile([P, N_TILE], F32, name="acc")
+            nc.tensor.matmul(out=spread[:], lhsT=ones[:], rhs=bias_rows[:, cols], start=True, stop=True)
+            nc.scalar.copy(out=bias_all[:, cols], in_=spread[:])
+
+        def add_bias(pos, name):
+            addend = keep.tile([P, EMBED], F32, name=name)
+            for n in range(EMBED // N_TILE):
+                cols = slice(N_TILE * n, N_TILE * (n + 1))
+                nc.gpsimd.tensor_tensor(out=addend[:, cols], in0=bias_all[:, cols], in1=pos[:, cols], op=ADD)
+            return addend
+
+        addend_wide = [add_bias(pos_wide[0], "addend_wide0")]
+
+        grouped_wide = [
+            keep.tile([P, BATCH, WIDE_CELLS, TUBES, PACK], BF16, align_bytes=64, name="grouped_wide%d" % h)
+            for h in range(2)
+        ]
+        grouped_tail = keep.tile([P, BATCH, TUBES, TAIL_CELLS, PACK], BF16, align_bytes=64)
+
+        def place_of_cell(cell):
+            if cell < 2 * WIDE_CELLS:
+                return grouped_wide[cell // WIDE_CELLS][:].bitcast(F32)[:, :, cell % WIDE_CELLS, :, :]
+            return grouped_tail[:].bitcast(F32)[:, :, :, cell - 2 * WIDE_CELLS, :]
+
+        def features_to_partitions(patch_rows, cells, on_vector):
+            token = sort_pool.tile([P, PATCH_ROWS * PATCH], BF16, name="token")
+            nc.vector.tensor_copy(out=token[:].rearrange("p (r w) -> p r w", w=PATCH), in_=patch_rows)
+            words = token[:].bitcast(F32)
+            flipped = flip_pool.tile([P, 2, P], F32, name="flipped")
+            for u in range(2):
+                nc.tensor.transpose(flipped[:, u, :], words[:, u : 2 * P : 2], ident[:])
+            by_cell = flipped[:].rearrange("p u (b d m) -> p m b d u", b=BATCH, d=TUBES)
+            for m in range(len(cells)):
+                if on_vector:
+                    nc.vector.tensor_copy(out=place_of_cell(cells[m]), in_=by_cell[:, m])
+                else:
+                    nc.scalar.copy(out=place_of_cell(cells[m]), in_=by_cell[:, m])
+
+        def quantise(grouped, tokens, name):
+            codes = keep.tile([P, tokens], U32, align_bytes=64, name="codes_" + name)
+            scales = keep.tile([P, tokens], U8, align_bytes=64, name="scales_" + name)
+            nc.vector.quantize_mx(out=codes[:].bitcast(FP8X4), scales=scales[:], in_=grouped)
+            return codes, scales
+
+        def project(codes, scales, first, addend, out_rows):
+            tokens = slice(first, first + P)
+            for n in range(EMBED // N_TILE):
+                cols = slice(N_TILE * n, N_TILE * (n + 1))
+                acc = acc_pool.tile([P, N_TILE], F32, name="acc")
+                nc.tensor.matmul_mx(
+                    out=acc[:],
+                    lhsT=codes[:, tokens].bitcast(FP8X4),
+                    lhsT_scale=scales[:, tokens],
+                    rhs=w_words[:, 2 * N_TILE * n : 2 * N_TILE * (n + 1)].bitcast(FP4X4),
+                    rhs_scale=w_scales[:, cols],
+                    start=True,
+                    stop=True,
+                )
+                result = result_pool.tile([P, N_TILE], F32, name="result")
+                nc.vector.tensor_tensor(out=result[:], in0=acc[:], in1=addend[:, cols], op=ADD)
+                nc.sync.dma_start(out=out_rows[:, :, cols], in_=result[:])
+
+        patches_a = rows_a[:].rearrange("p t (y j w) -> p (t y) j w", j=GRID, w=PATCH)
+        for j in range(GRID):
+            features_to_partitions(
+                patches_a[:, :, j, :], [GRID * i + j for i in range(ROWS_A)], on_vector=(j % 2 == 1)
+            )
+
+        codes0, scales0 = quantise(grouped_wide[0][:].rearrange("p b c d t -> p (b c d t)"), BATCH * P, "wide0")
+        for batch in range(BATCH):
+            project(codes0, scales0, P * batch, addend_wide[0], out_by_cell[batch, 0:WIDE_CELLS])
+
+        patches_b = rows_b[:].rearrange("p t (y s w) -> p (t y) s w", s=GRID // 2, w=2 * PATCH)
+        for s in range(GRID // 2):
+            features_to_partitions(
+                patches_b[:, :, s, 0:PATCH],
+                [GRID * i + 2 * s + shift for i in range(ROWS_A, GRID) for shift in range(2)],
+                on_vector=False,
+            )
+
+        addend_wide.append(add_bias(pos_wide[1], "addend_wide1"))
+        addend_tail = add_bias(pos_tail, "addend_tail")
+
+        codes1, scales1 = quantise(grouped_wide[1][:].rearrange("p b c d t -> p (b c d t)"), BATCH * P, "wide1")
+        for batch in range(BATCH):
+            project(codes1, scales1, P * batch, addend_wide[1], out_by_cell[batch, WIDE_CELLS : 2 * WIDE_CELLS])
+        codes2, scales2 = quantise(grouped_tail[:].rearrange("p b d c t -> p (b d c t)"), P, "tail")
+        project(codes2, scales2, 0, addend_tail, out_by_clip[:, 2 * WIDE_CELLS : CELLS])

@@ -36,10 +36,9 @@ def tile_tubeletembedding_kernel(tc, video, W_words, W_scales, b, pos_embed, out
     nc = tc.nc
     with ExitStack() as ctx:
         keep = ctx.enter_context(tc.tile_pool(name="keep", bufs=1))
-        sort_pool = ctx.enter_context(tc.tile_pool(name="sort", bufs=4))
+        sort_pool = ctx.enter_context(tc.tile_pool(name="sort", bufs=9))
         result_pool = ctx.enter_context(tc.tile_pool(name="result", bufs=6))
-        flip_pool = ctx.enter_context(tc.psum_pool(name="flip", bufs=4))
-        acc_pool = ctx.enter_context(tc.psum_pool(name="acc", bufs=4))
+        bank_pool = ctx.enter_context(tc.psum_pool(name="bank", bufs=8))
 
         bands = video.rearrange("b f c h w -> (b f c h w)").rearrange(
             "(x t i r) -> t x i r", x=CLIPS, t=FRAMES, i=GRID, r=BAND
@@ -57,11 +56,25 @@ def tile_tubeletembedding_kernel(tc, video, W_words, W_scales, b, pos_embed, out
         nc.vector.memset(bias_rows[:], 0.0)
         w_scales = keep.tile([P, EMBED], U8, align_bytes=64)
         nc.vector.memset(w_scales[:].bitcast(I32), 0)
+        perm_a = keep.tile([P, P], F32)
+        nc.vector.tensor_copy(
+            out=perm_a[:].rearrange("p (b m d) -> p b m d", b=BATCH, m=4),
+            in_=ident[:].rearrange("p (b d m) -> p b m d", b=BATCH, m=4),
+        )
+        perm_b = keep.tile([P, P], F32)
+        nc.vector.tensor_copy(
+            out=perm_b[:, 0:64].rearrange("p (b h d) -> p b h d", b=BATCH, h=2),
+            in_=ident[:].rearrange("p (b d i h) -> p i b h d", b=BATCH, i=2, h=2)[:, 0],
+        )
+        nc.vector.tensor_copy(
+            out=perm_b[:, 64:128].rearrange("p (b d h) -> p b d h", b=BATCH, h=2),
+            in_=ident[:].rearrange("p (b d i h) -> p i b d h", b=BATCH, i=2, h=2)[:, 1],
+        )
 
+        nc.sync.dma_start(out=bias_rows[0:1, :], in_=b.rearrange("(o e) -> o e", o=1))
         rows_a = keep.tile([P, FRAMES, BAND], BF16)
         for t in range(FRAMES):
             nc.sync.dma_start(out=rows_a[:, t, :], in_=bands[t, :, 0:ROWS_A, :])
-        nc.sync.dma_start(out=bias_rows[0:1, :], in_=b.rearrange("(o e) -> o e", o=1))
         for quadrant in range(4):
             nc.sync.dma_start(
                 out=w_scales[32 * quadrant : 32 * quadrant + 4, :].bitcast(I32),
@@ -91,7 +104,7 @@ def tile_tubeletembedding_kernel(tc, video, W_words, W_scales, b, pos_embed, out
         bias_all = keep.tile([P, EMBED], F32)
         for n in range(EMBED // N_TILE):
             cols = slice(N_TILE * n, N_TILE * (n + 1))
-            spread = acc_pool.tile([P, N_TILE], F32, name="acc")
+            spread = bank_pool.tile([P, N_TILE], F32, name="bank")
             nc.tensor.matmul(out=spread[:], lhsT=ones[:], rhs=bias_rows[:, cols], start=True, stop=True)
             nc.scalar.copy(out=bias_all[:, cols], in_=spread[:])
 
@@ -109,37 +122,34 @@ def tile_tubeletembedding_kernel(tc, video, W_words, W_scales, b, pos_embed, out
             for h in range(2)
         ]
         grouped_tail = keep.tile([P, BATCH, TUBES, TAIL_CELLS, PACK], BF16, align_bytes=64)
+        wide_words = [g[:].bitcast(F32) for g in grouped_wide]
+        tail_words = grouped_tail[:].bitcast(F32)
 
-        def place_of_cell(cell):
-            if cell < 2 * WIDE_CELLS:
-                return grouped_wide[cell // WIDE_CELLS][:].bitcast(F32)[:, :, cell % WIDE_CELLS, :, :]
-            return grouped_tail[:].bitcast(F32)[:, :, :, cell - 2 * WIDE_CELLS, :]
+        def copy_on(engine, out_, in_):
+            if engine == "v":
+                nc.vector.tensor_copy(out=out_, in_=in_)
+            else:
+                nc.scalar.copy(out=out_, in_=in_)
 
-        def features_to_partitions(patch_rows, cells, on_vector):
-            token = sort_pool.tile([P, PATCH_ROWS * PATCH], BF16, name="token")
-            nc.vector.tensor_copy(out=token[:].rearrange("p (r w) -> p r w", w=PATCH), in_=patch_rows)
-            words = token[:].bitcast(F32)
-            flipped = flip_pool.tile([P, 2, P], F32, name="flipped")
+        def sort(words, engine):
+            token = sort_pool.tile([P, 2, P], F32, name="token")
+            copy_on(engine, token[:].rearrange("p u (r w) -> p u r w", w=4), words)
+            return token
+
+        def flip(token, perm):
+            flipped = bank_pool.tile([P, 2, P], F32, name="bank")
             for u in range(2):
-                nc.tensor.transpose(flipped[:, u, :], words[:, u : 2 * P : 2], ident[:])
-            by_cell = flipped[:].rearrange("p u (b d m) -> p m b d u", b=BATCH, d=TUBES)
-            for m in range(len(cells)):
-                if on_vector:
-                    nc.vector.tensor_copy(out=place_of_cell(cells[m]), in_=by_cell[:, m])
-                else:
-                    nc.scalar.copy(out=place_of_cell(cells[m]), in_=by_cell[:, m])
+                nc.tensor.transpose(flipped[:, u, :], token[:, u, :], perm[:])
+            return flipped
 
-        def quantise(grouped, tokens, name):
-            codes = keep.tile([P, tokens], U32, align_bytes=64, name="codes_" + name)
-            scales = keep.tile([P, tokens], U8, align_bytes=64, name="scales_" + name)
-            nc.vector.quantize_mx(out=codes[:].bitcast(FP8X4), scales=scales[:], in_=grouped)
-            return codes, scales
+        def quantise(grouped, codes, scales):
+            nc.vector.quantize_mx(out=codes.bitcast(FP8X4), scales=scales, in_=grouped)
 
         def project(codes, scales, first, addend, out_rows):
             tokens = slice(first, first + P)
             for n in range(EMBED // N_TILE):
                 cols = slice(N_TILE * n, N_TILE * (n + 1))
-                acc = acc_pool.tile([P, N_TILE], F32, name="acc")
+                acc = bank_pool.tile([P, N_TILE], F32, name="bank")
                 nc.tensor.matmul_mx(
                     out=acc[:],
                     lhsT=codes[:, tokens].bitcast(FP8X4),
@@ -153,29 +163,72 @@ def tile_tubeletembedding_kernel(tc, video, W_words, W_scales, b, pos_embed, out
                 nc.vector.tensor_tensor(out=result[:], in0=acc[:], in1=addend[:, cols], op=ADD)
                 nc.sync.dma_start(out=out_rows[:, :, cols], in_=result[:])
 
-        patches_a = rows_a[:].rearrange("p t (y j w) -> p (t y) j w", j=GRID, w=PATCH)
+        words_a = (
+            rows_a[:]
+            .rearrange("p t r -> p (t r)")
+            .bitcast(F32)
+            .rearrange("p (r j w u) -> p j u r w", j=GRID, w=4, u=2)
+        )
+        words_b = (
+            rows_b[:]
+            .rearrange("p t r -> p (t r)")
+            .bitcast(F32)
+            .rearrange("p (r s h w u) -> p s h u r w", s=GRID // 2, h=2, w=4, u=2)
+        )
+
+        tokens_a = [sort(words_a[:, j], "v" if j % 2 == 0 else "s") for j in range(GRID)]
         for j in range(GRID):
-            features_to_partitions(
-                patches_a[:, :, j, :], [GRID * i + j for i in range(ROWS_A)], on_vector=(j % 2 == 1)
+            flipped = flip(tokens_a[j], perm_a)
+            view = flipped[:].rearrange("p u (b m d) -> p b m d u", b=BATCH, m=4)
+            low = 3 if j < 4 else 2
+            engine = "s" if j % 2 == 0 else "v"
+            copy_on(engine, wide_words[0][:, :, j : j + GRID * (low - 1) + 1 : GRID, :, :], view[:, :, 0:low])
+            first = GRID * low + j - WIDE_CELLS
+            copy_on(
+                engine,
+                wide_words[1][:, :, first : first + GRID * (ROWS_A - low - 1) + 1 : GRID, :, :],
+                view[:, :, low:ROWS_A],
             )
 
-        codes0, scales0 = quantise(grouped_wide[0][:].rearrange("p b c d t -> p (b c d t)"), BATCH * P, "wide0")
-        for batch in range(BATCH):
-            project(codes0, scales0, P * batch, addend_wide[0], out_by_cell[batch, 0:WIDE_CELLS])
+        tokens_b = [sort(words_b[:, s, 0], "s") for s in range(GRID // 2)]
 
-        patches_b = rows_b[:].rearrange("p t (y s w) -> p (t y) s w", s=GRID // 2, w=2 * PATCH)
-        for s in range(GRID // 2):
-            features_to_partitions(
-                patches_b[:, :, s, 0:PATCH],
-                [GRID * i + 2 * s + shift for i in range(ROWS_A, GRID) for shift in range(2)],
-                on_vector=False,
+        codes = [keep.tile([P, BATCH * P], U32, align_bytes=64, name="codes%d" % h) for h in range(2)]
+        scales = [keep.tile([P, BATCH * P], U8, align_bytes=64, name="scales%d" % h) for h in range(2)]
+
+        def quantise_wide(h, half):
+            cols = slice(2 * P * half, 2 * P * (half + 1))
+            quantise(
+                grouped_wide[h][:, 2 * half : 2 * half + 2].rearrange("p b c d t -> p (b c d t)"),
+                codes[h][:, cols],
+                scales[h][:, cols],
             )
 
+        def flip_b(s):
+            flipped = flip(tokens_b[s], perm_a if s == 0 else perm_b)
+            if s == 0:
+                view = flipped[:].rearrange("p u (b i h d) -> p b i h d u", b=BATCH, i=2, h=2)
+                copy_on("s", wide_words[1][:, :, 8:10, :, :], view[:, :, 0])
+                copy_on("s", wide_words[1][:, :, 14:16, :, :], view[:, :, 1])
+            else:
+                view = flipped[:, :, 0:64].rearrange("p u (b h d) -> p b h d u", b=BATCH, h=2)
+                copy_on("s", wide_words[1][:, :, 8 + 2 * s : 10 + 2 * s, :, :], view)
+                view = flipped[:, :, 64:128].rearrange("p u (b d h) -> p b d h u", b=BATCH, h=2)
+                copy_on("s", tail_words[:, :, :, 2 * s - 2 : 2 * s, :], view)
+
+        quantise_wide(0, 0)
+        quantise_wide(0, 1)
         addend_wide.append(add_bias(pos_wide[1], "addend_wide1"))
         addend_tail = add_bias(pos_tail, "addend_tail")
-
-        codes1, scales1 = quantise(grouped_wide[1][:].rearrange("p b c d t -> p (b c d t)"), BATCH * P, "wide1")
         for batch in range(BATCH):
-            project(codes1, scales1, P * batch, addend_wide[1], out_by_cell[batch, WIDE_CELLS : 2 * WIDE_CELLS])
-        codes2, scales2 = quantise(grouped_tail[:].rearrange("p b d c t -> p (b d c t)"), P, "tail")
+            project(codes[0], scales[0], P * batch, addend_wide[0], out_by_cell[batch, 0:WIDE_CELLS])
+            if batch < GRID // 2:
+                flip_b(batch)
+
+        quantise_wide(1, 0)
+        quantise_wide(1, 1)
+        codes2 = keep.tile([P, P], U32, align_bytes=64)
+        scales2 = keep.tile([P, P], U8, align_bytes=64)
+        quantise(grouped_tail[:].rearrange("p b d c t -> p (b d c t)"), codes2[:], scales2[:])
+        for batch in range(BATCH):
+            project(codes[1], scales[1], P * batch, addend_wide[1], out_by_cell[batch, WIDE_CELLS : 2 * WIDE_CELLS])
         project(codes2, scales2, 0, addend_tail, out_by_clip[:, 2 * WIDE_CELLS : CELLS])

@@ -39,6 +39,7 @@ def tile_tubeletembedding_kernel(tc, video, W_words, W_scales, b, pos_embed, out
         sort_pool = ctx.enter_context(tc.tile_pool(name="sort", bufs=9))
         result_pool = ctx.enter_context(tc.tile_pool(name="result", bufs=6))
         bank_pool = ctx.enter_context(tc.psum_pool(name="bank", bufs=8))
+        ctx.enter_context(tc.manual_schedule())
 
         bands = video.rearrange("b f c h w -> (b f c h w)").rearrange(
             "(x t i r) -> t x i r", x=CLIPS, t=FRAMES, i=GRID, r=BAND
@@ -50,10 +51,12 @@ def tile_tubeletembedding_kernel(tc, video, W_words, W_scales, b, pos_embed, out
 
         ident = keep.tile([P, P], F32)
         make_identity(nc, ident[:])
-        ones = keep.tile([P, P], BF16)
-        nc.vector.memset(ones[:], 1.0)
         bias_rows = keep.tile([P, EMBED], BF16)
         nc.vector.memset(bias_rows[:], 0.0)
+        ones = keep.tile([P, P], BF16)
+        nc.vector.memset(ones[:], 1.0)
+        warm = keep.tile([P, 1], BF16)
+        nc.scalar.copy(out=warm[:], in_=ones[:, 0:1])
         w_scales = keep.tile([P, EMBED], U8, align_bytes=64)
         nc.vector.memset(w_scales[:].bitcast(I32), 0)
         perm_a = keep.tile([P, P], F32)
@@ -71,20 +74,20 @@ def tile_tubeletembedding_kernel(tc, video, W_words, W_scales, b, pos_embed, out
             in_=ident[:].rearrange("p (b d i h) -> p i b d h", b=BATCH, i=2, h=2)[:, 1],
         )
 
-        nc.sync.dma_start(out=bias_rows[0:1, :], in_=b.rearrange("(o e) -> o e", o=1))
         rows_a = keep.tile([P, FRAMES, BAND], BF16)
-        for t in range(FRAMES):
-            nc.sync.dma_start(out=rows_a[:, t, :], in_=bands[t, :, 0:ROWS_A, :])
+        nc.sync.dma_start(out=rows_a[:, 0, :], in_=bands[0, :, 0:ROWS_A, :])
+        nc.sync.dma_start(out=bias_rows[0:1, :], in_=b.rearrange("(o e) -> o e", o=1))
+        nc.sync.dma_start(out=rows_a[:, 1, :], in_=bands[1, :, 0:ROWS_A, :])
+        pos_wide = []
+        pos_wide.append(keep.tile([P, EMBED], BF16, name="pos_wide0"))
+        nc.sync.dma_start(out=pos_wide[0][:], in_=pos_by_cell[0:WIDE_CELLS])
+        w_words = keep.tile([P, 2 * EMBED], U8, align_bytes=64)
+        nc.sync.dma_start(out=w_words[:].bitcast(I32), in_=W_words[0].bitcast(I32))
         for quadrant in range(4):
             nc.sync.dma_start(
                 out=w_scales[32 * quadrant : 32 * quadrant + 4, :].bitcast(I32),
                 in_=W_scales[0, 4 * quadrant : 4 * quadrant + 4, :].bitcast(I32),
             )
-        w_words = keep.tile([P, 2 * EMBED], U8, align_bytes=64)
-        nc.sync.dma_start(out=w_words[:].bitcast(I32), in_=W_words[0].bitcast(I32))
-        pos_wide = []
-        pos_wide.append(keep.tile([P, EMBED], BF16, name="pos_wide0"))
-        nc.sync.dma_start(out=pos_wide[0][:], in_=pos_by_cell[0:WIDE_CELLS])
         rows_b = keep.tile([P, FRAMES, BAND], BF16)
         for t in range(FRAMES):
             for shift in range(2):
@@ -181,7 +184,7 @@ def tile_tubeletembedding_kernel(tc, video, W_words, W_scales, b, pos_embed, out
             flipped = flip(tokens_a[j], perm_a)
             view = flipped[:].rearrange("p u (b m d) -> p b m d u", b=BATCH, m=4)
             low = 3 if j < 4 else 2
-            engine = "s" if j % 2 == 0 else "v"
+            engine = "v" if j % 2 == 0 else "s"
             copy_on(engine, wide_words[0][:, :, j : j + GRID * (low - 1) + 1 : GRID, :, :], view[:, :, 0:low])
             first = GRID * low + j - WIDE_CELLS
             copy_on(
@@ -221,8 +224,8 @@ def tile_tubeletembedding_kernel(tc, video, W_words, W_scales, b, pos_embed, out
         addend_tail = add_bias(pos_tail, "addend_tail")
         for batch in range(BATCH):
             project(codes[0], scales[0], P * batch, addend_wide[0], out_by_cell[batch, 0:WIDE_CELLS])
-            if batch < GRID // 2:
-                flip_b(batch)
+        for s in range(GRID // 2):
+            flip_b(s)
 
         quantise_wide(1, 0)
         quantise_wide(1, 1)

@@ -74,6 +74,14 @@ def tile_tubeletembedding_kernel(tc, video, W_words, W_scales, b, pos_embed, out
             in_=ident[:].rearrange("p (b d i h) -> p i b d h", b=BATCH, i=2, h=2)[:, 1],
         )
 
+        tail_rows = keep.tile([P, EMBED], BF16)
+        nc.vector.memset(tail_rows[:], 0.0)
+        pick = keep.tile([P, P], BF16)
+        nc.vector.memset(pick[:], 0.0)
+        nc.vector.memset(pick[32:33, :], 1.0)
+        for batch in range(BATCH):
+            nc.vector.tensor_copy(out=pick[0:32, 32 * batch : 32 * (batch + 1)], in_=ident[0:32, 0:32])
+
         rows_a = keep.tile([P, FRAMES, BAND], BF16)
         nc.sync.dma_start(out=rows_a[:, 0, :], in_=bands[0, :, 0:ROWS_A, :])
         nc.sync.dma_start(out=bias_rows[0:1, :], in_=b.rearrange("(o e) -> o e", o=1))
@@ -97,12 +105,8 @@ def tile_tubeletembedding_kernel(tc, video, W_words, W_scales, b, pos_embed, out
                 )
         pos_wide.append(keep.tile([P, EMBED], BF16, name="pos_wide1"))
         nc.sync.dma_start(out=pos_wide[1][:], in_=pos_by_cell[WIDE_CELLS : 2 * WIDE_CELLS])
-        pos_tail = keep.tile([P, EMBED], BF16)
-        for batch in range(BATCH):
-            nc.sync.dma_start(
-                out=pos_tail[TUBES * TAIL_CELLS * batch : TUBES * TAIL_CELLS * (batch + 1), :],
-                in_=pos_by_tube[:, 2 * WIDE_CELLS : CELLS, :],
-            )
+        nc.sync.dma_start(out=tail_rows[0 : TUBES * TAIL_CELLS, :], in_=pos_by_tube[:, 2 * WIDE_CELLS : CELLS, :])
+        nc.sync.dma_start(out=tail_rows[32:33, :], in_=b.rearrange("(o e) -> o e", o=1))
 
         bias_all = keep.tile([P, EMBED], F32)
         for n in range(EMBED // N_TILE):
@@ -221,11 +225,16 @@ def tile_tubeletembedding_kernel(tc, video, W_words, W_scales, b, pos_embed, out
         quantise_wide(0, 0)
         quantise_wide(0, 1)
         addend_wide.append(add_bias(pos_wide[1], "addend_wide1"))
-        addend_tail = add_bias(pos_tail, "addend_tail")
         for batch in range(BATCH):
             project(codes[0], scales[0], P * batch, addend_wide[0], out_by_cell[batch, 0:WIDE_CELLS])
         for s in range(GRID // 2):
             flip_b(s)
+        addend_tail = keep.tile([P, EMBED], F32)
+        for n in range(EMBED // N_TILE):
+            cols = slice(N_TILE * n, N_TILE * (n + 1))
+            spread = bank_pool.tile([P, N_TILE], F32, name="bank")
+            nc.tensor.matmul(out=spread[:], lhsT=pick[:], rhs=tail_rows[:, cols], start=True, stop=True)
+            nc.scalar.copy(out=addend_tail[:, cols], in_=spread[:])
 
         quantise_wide(1, 0)
         quantise_wide(1, 1)

@@ -37,7 +37,7 @@ def tile_tubeletembedding_kernel(tc, video, W_words, W_scales, b, pos_embed, out
     with ExitStack() as ctx:
         keep = ctx.enter_context(tc.tile_pool(name="keep", bufs=1))
         sort_pool = ctx.enter_context(tc.tile_pool(name="sort", bufs=9))
-        result_pool = ctx.enter_context(tc.tile_pool(name="result", bufs=6))
+        result_pool = ctx.enter_context(tc.tile_pool(name="result", bufs=8))
         bank_pool = ctx.enter_context(tc.psum_pool(name="bank", bufs=8))
         ctx.enter_context(tc.manual_schedule())
 
@@ -152,7 +152,7 @@ def tile_tubeletembedding_kernel(tc, video, W_words, W_scales, b, pos_embed, out
         def quantise(grouped, codes, scales):
             nc.vector.quantize_mx(out=codes.bitcast(FP8X4), scales=scales, in_=grouped)
 
-        def project(codes, scales, first, addend, out_rows):
+        def project(codes, scales, first, addend, out_rows, pieces=(1, 1)):
             tokens = slice(first, first + P)
             for n in range(EMBED // N_TILE):
                 cols = slice(N_TILE * n, N_TILE * (n + 1))
@@ -166,9 +166,14 @@ def tile_tubeletembedding_kernel(tc, video, W_words, W_scales, b, pos_embed, out
                     start=True,
                     stop=True,
                 )
-                result = result_pool.tile([P, N_TILE], F32, name="result")
-                nc.vector.tensor_tensor(out=result[:], in0=acc[:], in1=addend[:, cols], op=ADD)
-                nc.sync.dma_start(out=out_rows[:, :, cols], in_=result[:])
+                width = N_TILE // pieces[n]
+                for k in range(pieces[n]):
+                    part = slice(N_TILE * n + width * k, N_TILE * n + width * (k + 1))
+                    result = result_pool.tile([P, width], F32, name="result")
+                    nc.vector.tensor_tensor(
+                        out=result[:], in0=acc[:, width * k : width * (k + 1)], in1=addend[:, part], op=ADD
+                    )
+                    nc.sync.dma_start(out=out_rows[:, :, part], in_=result[:])
 
         words_a = (
             rows_a[:]
@@ -184,17 +189,21 @@ def tile_tubeletembedding_kernel(tc, video, W_words, W_scales, b, pos_embed, out
         )
 
         tokens_a = [sort(words_a[:, j], "v" if j % 2 == 0 else "s") for j in range(GRID)]
+        views_a = []
         for j in range(GRID):
             flipped = flip(tokens_a[j], perm_a)
             view = flipped[:].rearrange("p u (b m d) -> p b m d u", b=BATCH, m=4)
+            views_a.append(view)
             low = 3 if j < 4 else 2
             engine = "v" if j % 2 == 0 else "s"
             copy_on(engine, wide_words[0][:, :, j : j + GRID * (low - 1) + 1 : GRID, :, :], view[:, :, 0:low])
+        for j in range(GRID):
+            low = 3 if j < 4 else 2
             first = GRID * low + j - WIDE_CELLS
             copy_on(
-                engine,
+                "s",
                 wide_words[1][:, :, first : first + GRID * (ROWS_A - low - 1) + 1 : GRID, :, :],
-                view[:, :, low:ROWS_A],
+                views_a[j][:, :, low:ROWS_A],
             )
 
         tokens_b = [sort(words_b[:, s, 0], "s") for s in range(GRID // 2)]
@@ -202,10 +211,10 @@ def tile_tubeletembedding_kernel(tc, video, W_words, W_scales, b, pos_embed, out
         codes = [keep.tile([P, BATCH * P], U32, align_bytes=64, name="codes%d" % h) for h in range(2)]
         scales = [keep.tile([P, BATCH * P], U8, align_bytes=64, name="scales%d" % h) for h in range(2)]
 
-        def quantise_wide(h, half):
-            cols = slice(2 * P * half, 2 * P * (half + 1))
+        def quantise_wide(h, first, count):
+            cols = slice(P * first, P * (first + count))
             quantise(
-                grouped_wide[h][:, 2 * half : 2 * half + 2].rearrange("p b c d t -> p (b c d t)"),
+                grouped_wide[h][:, first : first + count].rearrange("p b c d t -> p (b c d t)"),
                 codes[h][:, cols],
                 scales[h][:, cols],
             )
@@ -222,11 +231,19 @@ def tile_tubeletembedding_kernel(tc, video, W_words, W_scales, b, pos_embed, out
                 view = flipped[:, :, 64:128].rearrange("p u (b d h) -> p b d h u", b=BATCH, h=2)
                 copy_on("s", tail_words[:, :, :, 2 * s - 2 : 2 * s, :], view)
 
-        quantise_wide(0, 0)
-        quantise_wide(0, 1)
+        quantise_wide(0, 0, 1)
+        quantise_wide(0, 1, 1)
+        quantise_wide(0, 2, 2)
         addend_wide.append(add_bias(pos_wide[1], "addend_wide1"))
         for batch in range(BATCH):
-            project(codes[0], scales[0], P * batch, addend_wide[0], out_by_cell[batch, 0:WIDE_CELLS])
+            project(
+                codes[0],
+                scales[0],
+                P * batch,
+                addend_wide[0],
+                out_by_cell[batch, 0:WIDE_CELLS],
+                pieces=(2, 1) if batch == 0 else (1, 1),
+            )
         for s in range(GRID // 2):
             flip_b(s)
         addend_tail = keep.tile([P, EMBED], F32)
@@ -236,8 +253,8 @@ def tile_tubeletembedding_kernel(tc, video, W_words, W_scales, b, pos_embed, out
             nc.tensor.matmul(out=spread[:], lhsT=pick[:], rhs=tail_rows[:, cols], start=True, stop=True)
             nc.scalar.copy(out=addend_tail[:, cols], in_=spread[:])
 
-        quantise_wide(1, 0)
-        quantise_wide(1, 1)
+        quantise_wide(1, 0, 2)
+        quantise_wide(1, 2, 2)
         codes2 = keep.tile([P, P], U32, align_bytes=64)
         scales2 = keep.tile([P, P], U8, align_bytes=64)
         quantise(grouped_tail[:].rearrange("p b d c t -> p (b d c t)"), codes2[:], scales2[:])

@@ -74,13 +74,8 @@ def tile_tubeletembedding_kernel(tc, video, W_words, W_scales, b, pos_embed, out
             in_=ident[:].rearrange("p (b d i h) -> p i b d h", b=BATCH, i=2, h=2)[:, 1],
         )
 
-        tail_rows = keep.tile([P, EMBED], BF16)
-        nc.vector.memset(tail_rows[:], 0.0)
-        pick = keep.tile([P, P], BF16)
-        nc.vector.memset(pick[:], 0.0)
-        nc.vector.memset(pick[32:33, :], 1.0)
-        for batch in range(BATCH):
-            nc.vector.tensor_copy(out=pick[0:32, 32 * batch : 32 * (batch + 1)], in_=ident[0:32, 0:32])
+        ident_bf = keep.tile([P, P], BF16)
+        nc.vector.tensor_copy(out=ident_bf[:], in_=ident[:])
 
         rows_a = keep.tile([P, FRAMES, BAND], BF16)
         nc.sync.dma_start(out=rows_a[:, 0, :], in_=bands[0, :, 0:ROWS_A, :])
@@ -105,31 +100,22 @@ def tile_tubeletembedding_kernel(tc, video, W_words, W_scales, b, pos_embed, out
                 )
         pos_wide.append(keep.tile([P, EMBED], BF16, name="pos_wide1"))
         nc.sync.dma_start(out=pos_wide[1][:], in_=pos_by_cell[WIDE_CELLS : 2 * WIDE_CELLS])
-        nc.sync.dma_start(out=tail_rows[0 : TUBES * TAIL_CELLS, :], in_=pos_by_tube[:, 2 * WIDE_CELLS : CELLS, :])
-        nc.sync.dma_start(out=tail_rows[32:33, :], in_=b.rearrange("(o e) -> o e", o=1))
+        pos_tail = keep.tile([P, EMBED], BF16)
+        for batch in range(BATCH):
+            nc.sync.dma_start(
+                out=pos_tail[32 * batch : 32 * (batch + 1), :], in_=pos_by_tube[:, 2 * WIDE_CELLS : CELLS, :]
+            )
 
-        bias_all = keep.tile([P, EMBED], F32)
-        for n in range(EMBED // N_TILE):
-            cols = slice(N_TILE * n, N_TILE * (n + 1))
-            spread = bank_pool.tile([P, N_TILE], F32, name="bank")
-            nc.tensor.matmul(out=spread[:], lhsT=ones[:], rhs=bias_rows[:, cols], start=True, stop=True)
-            nc.scalar.copy(out=bias_all[:, cols], in_=spread[:])
+        halves = [slice(N_TILE * n, N_TILE * (n + 1)) for n in range(EMBED // N_TILE)]
+        addend_banks = []
+        for cols in halves:
+            bank = bank_pool.tile([P, N_TILE], F32, name="bank")
+            nc.tensor.matmul(out=bank[:], lhsT=ones[:], rhs=bias_rows[:, cols], start=True, stop=False)
+            addend_banks.append(bank)
 
-        def add_bias(pos, name):
-            addend = keep.tile([P, EMBED], F32, name=name)
-            for n in range(EMBED // N_TILE):
-                cols = slice(N_TILE * n, N_TILE * (n + 1))
-                nc.gpsimd.tensor_tensor(out=addend[:, cols], in0=bias_all[:, cols], in1=pos[:, cols], op=ADD)
-            return addend
-
-        addend_wide = [add_bias(pos_wide[0], "addend_wide0")]
-
-        grouped_wide = [
-            keep.tile([P, BATCH, WIDE_CELLS, TUBES, PACK], BF16, align_bytes=64, name="grouped_wide%d" % h)
-            for h in range(2)
-        ]
+        grouped = keep.tile([P, BATCH, 2 * WIDE_CELLS, TUBES, PACK], BF16, align_bytes=64)
         grouped_tail = keep.tile([P, BATCH, TUBES, TAIL_CELLS, PACK], BF16, align_bytes=64)
-        wide_words = [g[:].bitcast(F32) for g in grouped_wide]
+        wide_words = grouped[:].bitcast(F32)
         tail_words = grouped_tail[:].bitcast(F32)
 
         def copy_on(engine, out_, in_):
@@ -149,31 +135,28 @@ def tile_tubeletembedding_kernel(tc, video, W_words, W_scales, b, pos_embed, out
                 nc.tensor.transpose(flipped[:, u, :], token[:, u, :], perm[:])
             return flipped
 
-        def quantise(grouped, codes, scales):
-            nc.vector.quantize_mx(out=codes.bitcast(FP8X4), scales=scales, in_=grouped)
+        def pass_mx(codes_, scales_, n):
+            acc = bank_pool.tile([P, N_TILE], F32, name="bank")
+            nc.tensor.matmul_mx(
+                out=acc[:],
+                lhsT=codes_.bitcast(FP8X4),
+                lhsT_scale=scales_,
+                rhs=w_words[:, 2 * N_TILE * n : 2 * N_TILE * (n + 1)].bitcast(FP4X4),
+                rhs_scale=w_scales[:, halves[n]],
+                start=True,
+                stop=True,
+            )
+            return acc
 
-        def project(codes, scales, first, addend, out_rows, pieces=(1, 1)):
-            tokens = slice(first, first + P)
-            for n in range(EMBED // N_TILE):
-                cols = slice(N_TILE * n, N_TILE * (n + 1))
-                acc = bank_pool.tile([P, N_TILE], F32, name="bank")
-                nc.tensor.matmul_mx(
-                    out=acc[:],
-                    lhsT=codes[:, tokens].bitcast(FP8X4),
-                    lhsT_scale=scales[:, tokens],
-                    rhs=w_words[:, 2 * N_TILE * n : 2 * N_TILE * (n + 1)].bitcast(FP4X4),
-                    rhs_scale=w_scales[:, cols],
-                    start=True,
-                    stop=True,
+        def finish(acc, n, addend, out_rows, pieces=1):
+            width = N_TILE // pieces
+            for k in range(pieces):
+                part = slice(N_TILE * n + width * k, N_TILE * n + width * (k + 1))
+                result = result_pool.tile([P, width], F32, name="result")
+                nc.vector.tensor_tensor(
+                    out=result[:], in0=acc[:, width * k : width * (k + 1)], in1=addend[:, part], op=ADD
                 )
-                width = N_TILE // pieces[n]
-                for k in range(pieces[n]):
-                    part = slice(N_TILE * n + width * k, N_TILE * n + width * (k + 1))
-                    result = result_pool.tile([P, width], F32, name="result")
-                    nc.vector.tensor_tensor(
-                        out=result[:], in0=acc[:, width * k : width * (k + 1)], in1=addend[:, part], op=ADD
-                    )
-                    nc.sync.dma_start(out=out_rows[:, :, part], in_=result[:])
+                nc.sync.dma_start(out=out_rows[:, :, part], in_=result[:])
 
         words_a = (
             rows_a[:]
@@ -189,75 +172,88 @@ def tile_tubeletembedding_kernel(tc, video, W_words, W_scales, b, pos_embed, out
         )
 
         tokens_a = [sort(words_a[:, j], "v" if j % 2 == 0 else "s") for j in range(GRID)]
-        views_a = []
         for j in range(GRID):
             flipped = flip(tokens_a[j], perm_a)
-            view = flipped[:].rearrange("p u (b m d) -> p b m d u", b=BATCH, m=4)
-            views_a.append(view)
-            low = 3 if j < 4 else 2
-            engine = "v" if j % 2 == 0 else "s"
-            copy_on(engine, wide_words[0][:, :, j : j + GRID * (low - 1) + 1 : GRID, :, :], view[:, :, 0:low])
-        for j in range(GRID):
-            low = 3 if j < 4 else 2
-            first = GRID * low + j - WIDE_CELLS
             copy_on(
-                "s",
-                wide_words[1][:, :, first : first + GRID * (ROWS_A - low - 1) + 1 : GRID, :, :],
-                views_a[j][:, :, low:ROWS_A],
+                "v" if j % 2 == 0 else "s",
+                wide_words[:, :, j : j + GRID * (ROWS_A - 1) + 1 : GRID, :, :],
+                flipped[:].rearrange("p u (b m d) -> p b m d u", b=BATCH, m=ROWS_A),
             )
+        addend_wide = [keep.tile([P, EMBED], F32, name="addend_wide%d" % h) for h in range(2)]
+        for n in range(2):
+            nc.tensor.matmul(
+                out=addend_banks[n][:], lhsT=ident_bf[:], rhs=pos_wide[0][:, halves[n]], start=False, stop=True
+            )
+            nc.scalar.copy(out=addend_wide[0][:, halves[n]], in_=addend_banks[n][:])
 
         tokens_b = [sort(words_b[:, s, 0], "s") for s in range(GRID // 2)]
 
-        codes = [keep.tile([P, BATCH * P], U32, align_bytes=64, name="codes%d" % h) for h in range(2)]
-        scales = [keep.tile([P, BATCH * P], U8, align_bytes=64, name="scales%d" % h) for h in range(2)]
+        codes = keep.tile([P, BATCH, 2, P], U32, align_bytes=64)
+        scales = keep.tile([P, BATCH, 2, P], U8, align_bytes=64)
 
-        def quantise_wide(h, first, count):
-            cols = slice(P * first, P * (first + count))
-            quantise(
-                grouped_wide[h][:, first : first + count].rearrange("p b c d t -> p (b c d t)"),
-                codes[h][:, cols],
-                scales[h][:, cols],
+        def quantise_wide(batch, h):
+            nc.vector.quantize_mx(
+                out=codes[:, batch, h, :].bitcast(FP8X4),
+                scales=scales[:, batch, h, :],
+                in_=grouped[:, batch, WIDE_CELLS * h : WIDE_CELLS * (h + 1)].rearrange("p c d t -> p (c d t)"),
             )
 
-        def flip_b(s):
+        def project_wide(batch, h, pieces=(1, 1)):
+            for n in range(2):
+                acc = pass_mx(codes[:, batch, h, :], scales[:, batch, h, :], n)
+                finish(
+                    acc,
+                    n,
+                    addend_wide[h],
+                    out_by_cell[batch, WIDE_CELLS * h : WIDE_CELLS * (h + 1)],
+                    pieces=pieces[n],
+                )
+
+        for batch in range(BATCH):
+            quantise_wide(batch, 0)
+        project_wide(0, 0, pieces=(2, 1))
+
+        bias_all = keep.tile([P, EMBED], F32)
+        for cols in halves:
+            spread = bank_pool.tile([P, N_TILE], F32, name="bank")
+            nc.tensor.matmul(out=spread[:], lhsT=ones[:], rhs=bias_rows[:, cols], start=True, stop=True)
+            nc.scalar.copy(out=bias_all[:, cols], in_=spread[:])
+        for cols in halves:
+            nc.gpsimd.tensor_tensor(
+                out=addend_wide[1][:, cols], in0=bias_all[:, cols], in1=pos_wide[1][:, cols], op=ADD
+            )
+
+        for batch in range(1, BATCH):
+            project_wide(batch, 0)
+
+        for s in range(GRID // 2):
             flipped = flip(tokens_b[s], perm_a if s == 0 else perm_b)
             if s == 0:
-                view = flipped[:].rearrange("p u (b i h d) -> p b i h d u", b=BATCH, i=2, h=2)
-                copy_on("s", wide_words[1][:, :, 8:10, :, :], view[:, :, 0])
-                copy_on("s", wide_words[1][:, :, 14:16, :, :], view[:, :, 1])
+                copy_on(
+                    "s",
+                    wide_words[:, :, 20:32, :, :].rearrange("p b (i c) d u -> p b i c d u", i=2)[:, :, :, 4:6],
+                    flipped[:].rearrange("p u (b i h d) -> p b i h d u", b=BATCH, i=2, h=2),
+                )
             else:
                 view = flipped[:, :, 0:64].rearrange("p u (b h d) -> p b h d u", b=BATCH, h=2)
-                copy_on("s", wide_words[1][:, :, 8 + 2 * s : 10 + 2 * s, :, :], view)
+                copy_on("s", wide_words[:, :, 24 + 2 * s : 26 + 2 * s, :, :], view)
                 view = flipped[:, :, 64:128].rearrange("p u (b d h) -> p b d h u", b=BATCH, h=2)
                 copy_on("s", tail_words[:, :, :, 2 * s - 2 : 2 * s, :], view)
 
-        quantise_wide(0, 0, 1)
-        quantise_wide(0, 1, 1)
-        quantise_wide(0, 2, 2)
-        addend_wide.append(add_bias(pos_wide[1], "addend_wide1"))
         for batch in range(BATCH):
-            project(
-                codes[0],
-                scales[0],
-                P * batch,
-                addend_wide[0],
-                out_by_cell[batch, 0:WIDE_CELLS],
-                pieces=(2, 1) if batch == 0 else (1, 1),
-            )
-        for s in range(GRID // 2):
-            flip_b(s)
-        addend_tail = keep.tile([P, EMBED], F32)
-        for n in range(EMBED // N_TILE):
-            cols = slice(N_TILE * n, N_TILE * (n + 1))
-            spread = bank_pool.tile([P, N_TILE], F32, name="bank")
-            nc.tensor.matmul(out=spread[:], lhsT=pick[:], rhs=tail_rows[:, cols], start=True, stop=True)
-            nc.scalar.copy(out=addend_tail[:, cols], in_=spread[:])
-
-        quantise_wide(1, 0, 2)
-        quantise_wide(1, 2, 2)
+            quantise_wide(batch, 1)
         codes2 = keep.tile([P, P], U32, align_bytes=64)
         scales2 = keep.tile([P, P], U8, align_bytes=64)
-        quantise(grouped_tail[:].rearrange("p b d c t -> p (b d c t)"), codes2[:], scales2[:])
+        nc.vector.quantize_mx(
+            out=codes2[:].bitcast(FP8X4), scales=scales2[:], in_=grouped_tail[:].rearrange("p b d c t -> p (b d c t)")
+        )
+        addend_tail = keep.tile([P, EMBED], F32)
+        nc.vector.memset(addend_tail[:, 0:2], 0.0)
+        for cols in halves:
+            nc.gpsimd.tensor_tensor(out=addend_tail[:, cols], in0=bias_all[:, cols], in1=pos_tail[:, cols], op=ADD)
+
         for batch in range(BATCH):
-            project(codes[1], scales[1], P * batch, addend_wide[1], out_by_cell[batch, WIDE_CELLS : 2 * WIDE_CELLS])
-        project(codes2, scales2, 0, addend_tail, out_by_clip[:, 2 * WIDE_CELLS : CELLS])
+            project_wide(batch, 1)
+        for n in range(2):
+            acc = pass_mx(codes2[:], scales2[:], n)
+            finish(acc, n, addend_tail, out_by_clip[:, 2 * WIDE_CELLS : CELLS])

@@ -135,18 +135,21 @@ def tile_tubeletembedding_kernel(tc, video, W_words, W_scales, b, pos_embed, out
                 nc.tensor.transpose(flipped[:, u, :], token[:, u, :], perm[:])
             return flipped
 
-        def pass_mx(codes_, scales_, n):
-            acc = bank_pool.tile([P, N_TILE], F32, name="bank")
+        def pass_cols(codes_, scales_, first, width):
+            acc = bank_pool.tile([P, width], F32, name="bank")
             nc.tensor.matmul_mx(
                 out=acc[:],
                 lhsT=codes_.bitcast(FP8X4),
                 lhsT_scale=scales_,
-                rhs=w_words[:, 2 * N_TILE * n : 2 * N_TILE * (n + 1)].bitcast(FP4X4),
-                rhs_scale=w_scales[:, halves[n]],
+                rhs=w_words[:, 2 * first : 2 * (first + width)].bitcast(FP4X4),
+                rhs_scale=w_scales[:, first : first + width],
                 start=True,
                 stop=True,
             )
             return acc
+
+        def pass_mx(codes_, scales_, n):
+            return pass_cols(codes_, scales_, N_TILE * n, N_TILE)
 
         def finish(acc, n, addend, out_rows, pieces=1):
             width = N_TILE // pieces
@@ -174,17 +177,24 @@ def tile_tubeletembedding_kernel(tc, video, W_words, W_scales, b, pos_embed, out
         tokens_a = [sort(words_a[:, j], "v" if j % 2 == 0 else "s") for j in range(GRID)]
         for j in range(GRID):
             flipped = flip(tokens_a[j], perm_a)
-            copy_on(
-                "v" if j % 2 == 0 else "s",
-                wide_words[:, :, j : j + GRID * (ROWS_A - 1) + 1 : GRID, :, :],
-                flipped[:].rearrange("p u (b m d) -> p b m d u", b=BATCH, m=ROWS_A),
-            )
+            cells = wide_words[:, :, j : j + GRID * (ROWS_A - 1) + 1 : GRID, :, :]
+            view = flipped[:].rearrange("p u (b m d) -> p b m d u", b=BATCH, m=ROWS_A)
+            if j < GRID - 1:
+                copy_on("v" if j % 2 == 0 else "s", cells, view)
+            else:
+                copy_on("s", cells[:, 0:1], view[:, 0:1])
+                copy_on("s", cells[:, 1:BATCH], view[:, 1:BATCH])
         addend_wide = [keep.tile([P, EMBED], F32, name="addend_wide%d" % h) for h in range(2)]
         for n in range(2):
             nc.tensor.matmul(
                 out=addend_banks[n][:], lhsT=ident_bf[:], rhs=pos_wide[0][:, halves[n]], start=False, stop=True
             )
-            nc.scalar.copy(out=addend_wide[0][:, halves[n]], in_=addend_banks[n][:])
+            for k in range(2 - n):
+                width = N_TILE // (2 - n)
+                nc.scalar.copy(
+                    out=addend_wide[0][:, N_TILE * n + width * k : N_TILE * n + width * (k + 1)],
+                    in_=addend_banks[n][:, width * k : width * (k + 1)],
+                )
 
         tokens_b = [sort(words_b[:, s, 0], "s") for s in range(GRID // 2)]
 
@@ -211,7 +221,14 @@ def tile_tubeletembedding_kernel(tc, video, W_words, W_scales, b, pos_embed, out
 
         for batch in range(BATCH):
             quantise_wide(batch, 0)
-        project_wide(0, 0, pieces=(2, 1))
+        for first in (0, N_TILE // 2):
+            acc = pass_cols(codes[:, 0, 0, :], scales[:, 0, 0, :], first, N_TILE // 2)
+            part = slice(first, first + N_TILE // 2)
+            result = result_pool.tile([P, N_TILE // 2], F32, name="result")
+            nc.vector.tensor_tensor(out=result[:], in0=acc[:], in1=addend_wide[0][:, part], op=ADD)
+            nc.sync.dma_start(out=out_by_cell[0, 0:WIDE_CELLS][:, :, part], in_=result[:])
+        acc = pass_mx(codes[:, 0, 0, :], scales[:, 0, 0, :], 1)
+        finish(acc, 1, addend_wide[0], out_by_cell[0, 0:WIDE_CELLS])
 
         bias_all = keep.tile([P, EMBED], F32)
         for cols in halves:

@@ -174,15 +174,22 @@ def tile_tubeletembedding_kernel(tc, video, W_words, W_scales, b, pos_embed, out
             .rearrange("p (r s h w u) -> p s h u r w", s=GRID // 2, h=2, w=4, u=2)
         )
 
-        tokens_a = [sort(words_a[:, j], "v" if j % 2 == 0 else "s") for j in range(GRID)]
+        tokens_a = [sort_pool.tile([P, 2, P], F32, name="token") for j in range(GRID)]
+        for t in range(FRAMES):
+            rows = slice(PATCH * t, PATCH * (t + 1))
+            for j in range(GRID):
+                nc.vector.tensor_copy(
+                    out=tokens_a[j][:].rearrange("p u (r w) -> p u r w", w=4)[:, :, rows, :],
+                    in_=words_a[:, j][:, :, rows, :],
+                )
         for j in range(GRID):
             flipped = flip(tokens_a[j], perm_a)
             cells = wide_words[:, :, j : j + GRID * (ROWS_A - 1) + 1 : GRID, :, :]
             view = flipped[:].rearrange("p u (b m d) -> p b m d u", b=BATCH, m=ROWS_A)
             if j < GRID - 1:
-                copy_on("v" if j % 2 == 0 else "s", cells, view)
+                copy_on("v" if j == GRID - 2 else "s", cells, view)
             else:
-                copy_on("s", cells[:, 0:1], view[:, 0:1])
+                copy_on("v", cells[:, 0:1], view[:, 0:1])
                 copy_on("s", cells[:, 1:BATCH], view[:, 1:BATCH])
         addend_wide = [keep.tile([P, EMBED], F32, name="addend_wide%d" % h) for h in range(2)]
         for n in range(2):

from contextlib import ExitStack

import concourse.mybir as mybir
from concourse.masks import make_identity

FLOPS = 2 * 1152 * 512 * 1024

BF16 = mybir.dt.bfloat16
F32 = mybir.dt.float32
I32 = mybir.dt.int32
U32 = mybir.dt.uint32
U8 = mybir.dt.uint8
FP8X4 = mybir.dt.float8_e4m3fn_x4
FP4X4 = mybir.dt.float4_e2m1fn_x4
ADD = mybir.AluOpType.add

P = 128
PACK = 4
BATCH = 4
TUBES = 8
CLIPS = BATCH * TUBES
FRAMES = 2
GRID = 6
PATCH = 16
BAND = PATCH * GRID * PATCH
CELLS = GRID * GRID
PATCH_ROWS = FRAMES * PATCH
EMBED = 1024
N_TILE = 512
WIDE_CELLS = 16
TAIL_CELLS = CELLS - 2 * WIDE_CELLS
ROWS_A = 4


def tile_tubeletembedding_kernel(tc, video, W_words, W_scales, b, pos_embed, out):
    nc = tc.nc
    with ExitStack() as ctx:
        keep = ctx.enter_context(tc.tile_pool(name="keep", bufs=1))
        sort_pool = ctx.enter_context(tc.tile_pool(name="sort", bufs=9))
        result_pool = ctx.enter_context(tc.tile_pool(name="result", bufs=8))
        bank_pool = ctx.enter_context(tc.psum_pool(name="bank", bufs=8))
        ctx.enter_context(tc.manual_schedule())

        bands = video.rearrange("b f c h w -> (b f c h w)").rearrange(
            "(x t i r) -> t x i r", x=CLIPS, t=FRAMES, i=GRID, r=BAND
        )
        pos_by_cell = pos_embed[0].rearrange("(d c) e -> c d e", c=CELLS)
        pos_by_tube = pos_embed[0].rearrange("(d c) e -> d c e", c=CELLS)
        out_by_cell = out.rearrange("b (d c) e -> b c d e", c=CELLS)
        out_by_clip = out.rearrange("b (d c) e -> (b d) c e", c=CELLS)

        ident = keep.tile([P, P], F32)
        make_identity(nc, ident[:])
        bias_rows = keep.tile([P, EMBED], BF16)
        nc.vector.memset(bias_rows[:], 0.0)
        ones = keep.tile([P, P], BF16)
        nc.vector.memset(ones[:], 1.0)
        warm = keep.tile([P, 1], BF16)
        nc.scalar.copy(out=warm[:], in_=ones[:, 0:1])
        w_scales = keep.tile([P, EMBED], U8, align_bytes=64)
        nc.vector.memset(w_scales[:].bitcast(I32), 0)
        perm_a = keep.tile([P, P], F32)
        nc.vector.tensor_copy(
            out=perm_a[:].rearrange("p (b m d) -> p b m d", b=BATCH, m=4),
            in_=ident[:].rearrange("p (b d m) -> p b m d", b=BATCH, m=4),
        )
        perm_b = keep.tile([P, P], F32)
        nc.vector.tensor_copy(
            out=perm_b[:, 0:64].rearrange("p (b h d) -> p b h d", b=BATCH, h=2),
            in_=ident[:].rearrange("p (b d i h) -> p i b h d", b=BATCH, i=2, h=2)[:, 0],
        )
        nc.vector.tensor_copy(
            out=perm_b[:, 64:128].rearrange("p (b d h) -> p b d h", b=BATCH, h=2),
            in_=ident[:].rearrange("p (b d i h) -> p i b d h", b=BATCH, i=2, h=2)[:, 1],
        )

        ident_bf = keep.tile([P, P], BF16)
        nc.vector.tensor_copy(out=ident_bf[:], in_=ident[:])

        rows_a = keep.tile([P, FRAMES, BAND], BF16)
        nc.sync.dma_start(out=rows_a[:, 0, :], in_=bands[0, :, 0:ROWS_A, :])
        nc.sync.dma_start(out=bias_rows[0:1, :], in_=b.rearrange("(o e) -> o e", o=1))
        nc.sync.dma_start(out=rows_a[:, 1, :], in_=bands[1, :, 0:ROWS_A, :])
        pos_wide = []
        pos_wide.append(keep.tile([P, EMBED], BF16, name="pos_wide0"))
        nc.sync.dma_start(out=pos_wide[0][:], in_=pos_by_cell[0:WIDE_CELLS])
        w_words = keep.tile([P, 2 * EMBED], U8, align_bytes=64)
        nc.sync.dma_start(out=w_words[:].bitcast(I32), in_=W_words[0].bitcast(I32))
        for quadrant in range(4):
            nc.sync.dma_start(
                out=w_scales[32 * quadrant : 32 * quadrant + 4, :].bitcast(I32),
                in_=W_scales[0, 4 * quadrant : 4 * quadrant + 4, :].bitcast(I32),
            )
        rows_b = keep.tile([P, FRAMES, BAND], BF16)
        for t in range(FRAMES):
            for shift in range(2):
                nc.sync.dma_start(
                    out=rows_b[shift:P:2, t, 0 : BAND - PATCH * shift],
                    in_=bands[t, :, ROWS_A:GRID, PATCH * shift : BAND],
                )
        pos_wide.append(keep.tile([P, EMBED], BF16, name="pos_wide1"))
        nc.sync.dma_start(out=pos_wide[1][:], in_=pos_by_cell[WIDE_CELLS : 2 * WIDE_CELLS])
        pos_tail = keep.tile([P, EMBED], BF16)
        for batch in range(BATCH):
            nc.sync.dma_start(
                out=pos_tail[32 * batch : 32 * (batch + 1), :], in_=pos_by_tube[:, 2 * WIDE_CELLS : CELLS, :]
            )

        halves = [slice(N_TILE * n, N_TILE * (n + 1)) for n in range(EMBED // N_TILE)]
        addend_banks = []
        for cols in halves:
            bank = bank_pool.tile([P, N_TILE], F32, name="bank")
            nc.tensor.matmul(out=bank[:], lhsT=ones[:], rhs=bias_rows[:, cols], start=True, stop=False)
            addend_banks.append(bank)

        grouped = keep.tile([P, BATCH, 2 * WIDE_CELLS, TUBES, PACK], BF16, align_bytes=64)
        grouped_tail = keep.tile([P, BATCH, TUBES, TAIL_CELLS, PACK], BF16, align_bytes=64)
        wide_words = grouped[:].bitcast(F32)
        tail_words = grouped_tail[:].bitcast(F32)

        def copy_on(engine, out_, in_):
            if engine == "v":
                nc.vector.tensor_copy(out=out_, in_=in_)
            else:
                nc.scalar.copy(out=out_, in_=in_)

        def sort(words, engine):
            token = sort_pool.tile([P, 2, P], F32, name="token")
            copy_on(engine, token[:].rearrange("p u (r w) -> p u r w", w=4), words)
            return token

        def flip(token, perm):
            flipped = bank_pool.tile([P, 2, P], F32, name="bank")
            for u in range(2):
                nc.tensor.transpose(flipped[:, u, :], token[:, u, :], perm[:])
            return flipped

        def pass_cols(codes_, scales_, first, width):
            acc = bank_pool.tile([P, width], F32, name="bank")
            nc.tensor.matmul_mx(
                out=acc[:],
                lhsT=codes_.bitcast(FP8X4),
                lhsT_scale=scales_,
                rhs=w_words[:, 2 * first : 2 * (first + width)].bitcast(FP4X4),
                rhs_scale=w_scales[:, first : first + width],
                start=True,
                stop=True,
            )
            return acc

        def pass_mx(codes_, scales_, n):
            return pass_cols(codes_, scales_, N_TILE * n, N_TILE)

        def finish(acc, n, addend, out_rows, pieces=1):
            width = N_TILE // pieces
            for k in range(pieces):
                part = slice(N_TILE * n + width * k, N_TILE * n + width * (k + 1))
                result = result_pool.tile([P, width], F32, name="result")
                nc.vector.tensor_tensor(
                    out=result[:], in0=acc[:, width * k : width * (k + 1)], in1=addend[:, part], op=ADD
                )
                nc.sync.dma_start(out=out_rows[:, :, part], in_=result[:])

        words_a = (
            rows_a[:]
            .rearrange("p t r -> p (t r)")
            .bitcast(F32)
            .rearrange("p (r j w u) -> p j u r w", j=GRID, w=4, u=2)
        )
        words_b = (
            rows_b[:]
            .rearrange("p t r -> p (t r)")
            .bitcast(F32)
            .rearrange("p (r s h w u) -> p s h u r w", s=GRID // 2, h=2, w=4, u=2)
        )

        tokens_a = [sort_pool.tile([P, 2, P], F32, name="token") for j in range(GRID)]
        for t in range(FRAMES):
            rows = slice(PATCH * t, PATCH * (t + 1))
            for j in range(GRID):
                nc.vector.tensor_copy(
                    out=tokens_a[j][:].rearrange("p u (r w) -> p u r w", w=4)[:, :, rows, :],
                    in_=words_a[:, j][:, :, rows, :],
                )
        for j in range(GRID):
            flipped = flip(tokens_a[j], perm_a)
            cells = wide_words[:, :, j : j + GRID * (ROWS_A - 1) + 1 : GRID, :, :]
            view = flipped[:].rearrange("p u (b m d) -> p b m d u", b=BATCH, m=ROWS_A)
            if j < GRID - 1:
                copy_on("v" if j == GRID - 2 else "s", cells, view)
            else:
                copy_on("v", cells[:, 0:1], view[:, 0:1])
                copy_on("s", cells[:, 1:BATCH], view[:, 1:BATCH])
        addend_wide = [keep.tile([P, EMBED], F32, name="addend_wide%d" % h) for h in range(2)]
        for n in range(2):
            nc.tensor.matmul(
                out=addend_banks[n][:], lhsT=ident_bf[:], rhs=pos_wide[0][:, halves[n]], start=False, stop=True
            )
            for k in range(2 - n):
                width = N_TILE // (2 - n)
                nc.scalar.copy(
                    out=addend_wide[0][:, N_TILE * n + width * k : N_TILE * n + width * (k + 1)],
                    in_=addend_banks[n][:, width * k : width * (k + 1)],
                )

        tokens_b = [sort(words_b[:, s, 0], "s") for s in range(GRID // 2)]

        codes = keep.tile([P, BATCH, 2, P], U32, align_bytes=64)
        scales = keep.tile([P, BATCH, 2, P], U8, align_bytes=64)

        def quantise_wide(batch, h):
            nc.vector.quantize_mx(
                out=codes[:, batch, h, :].bitcast(FP8X4),
                scales=scales[:, batch, h, :],
                in_=grouped[:, batch, WIDE_CELLS * h : WIDE_CELLS * (h + 1)].rearrange("p c d t -> p (c d t)"),
            )

        def project_wide(batch, h, pieces=(1, 1)):
            for n in range(2):
                acc = pass_mx(codes[:, batch, h, :], scales[:, batch, h, :], n)
                finish(
                    acc,
                    n,
                    addend_wide[h],
                    out_by_cell[batch, WIDE_CELLS * h : WIDE_CELLS * (h + 1)],
                    pieces=pieces[n],
                )

        for batch in range(BATCH):
            quantise_wide(batch, 0)
        for first in (0, N_TILE // 2):
            acc = pass_cols(codes[:, 0, 0, :], scales[:, 0, 0, :], first, N_TILE // 2)
            part = slice(first, first + N_TILE // 2)
            result = result_pool.tile([P, N_TILE // 2], F32, name="result")
            nc.vector.tensor_tensor(out=result[:], in0=acc[:], in1=addend_wide[0][:, part], op=ADD)
            nc.sync.dma_start(out=out_by_cell[0, 0:WIDE_CELLS][:, :, part], in_=result[:])
        acc = pass_mx(codes[:, 0, 0, :], scales[:, 0, 0, :], 1)
        finish(acc, 1, addend_wide[0], out_by_cell[0, 0:WIDE_CELLS])

        bias_all = keep.tile([P, EMBED], F32)
        for cols in halves:
            spread = bank_pool.tile([P, N_TILE], F32, name="bank")
            nc.tensor.matmul(out=spread[:], lhsT=ones[:], rhs=bias_rows[:, cols], start=True, stop=True)
            nc.scalar.copy(out=bias_all[:, cols], in_=spread[:])
        for cols in halves:
            nc.gpsimd.tensor_tensor(
                out=addend_wide[1][:, cols], in0=bias_all[:, cols], in1=pos_wide[1][:, cols], op=ADD
            )

        for batch in range(1, BATCH):
            project_wide(batch, 0)

        for s in range(GRID // 2):
            flipped = flip(tokens_b[s], perm_a if s == 0 else perm_b)
            if s == 0:
                copy_on(
                    "s",
                    wide_words[:, :, 20:32, :, :].rearrange("p b (i c) d u -> p b i c d u", i=2)[:, :, :, 4:6],
                    flipped[:].rearrange("p u (b i h d) -> p b i h d u", b=BATCH, i=2, h=2),
                )
            else:
                view = flipped[:, :, 0:64].rearrange("p u (b h d) -> p b h d u", b=BATCH, h=2)
                copy_on("s", wide_words[:, :, 24 + 2 * s : 26 + 2 * s, :, :], view)
                view = flipped[:, :, 64:128].rearrange("p u (b d h) -> p b d h u", b=BATCH, h=2)
                copy_on("s", tail_words[:, :, :, 2 * s - 2 : 2 * s, :], view)

        for batch in range(BATCH):
            quantise_wide(batch, 1)
        codes2 = keep.tile([P, P], U32, align_bytes=64)
        scales2 = keep.tile([P, P], U8, align_bytes=64)
        nc.vector.quantize_mx(
            out=codes2[:].bitcast(FP8X4), scales=scales2[:], in_=grouped_tail[:].rearrange("p b d c t -> p (b d c t)")
        )
        addend_tail = keep.tile([P, EMBED], F32)
        nc.vector.memset(addend_tail[:, 0:2], 0.0)
        for cols in halves:
            nc.gpsimd.tensor_tensor(out=addend_tail[:, cols], in0=bias_all[:, cols], in1=pos_tail[:, cols], op=ADD)

        for batch in range(BATCH):
            project_wide(batch, 1)
        for n in range(2):
            acc = pass_mx(codes2[:], scales2[:], n)
            finish(acc, n, addend_tail, out_by_clip[:, 2 * WIDE_CELLS : CELLS])
